import numpy as np
import ml_dtypes


def mxq(x, axis, fmt="e4m3"):
    dtype, down = {"e4m3": (ml_dtypes.float8_e4m3fn, 7), "e5m2": (ml_dtypes.float8_e5m2, 14)}[fmt]
    v = np.moveaxis(np.asarray(x, np.float32).astype(ml_dtypes.bfloat16).astype(np.float64), axis, -1)
    blocks = v.reshape(v.shape[:-1] + (-1, 32))
    amax = np.abs(blocks).max(-1, keepdims=True)
    byte = np.maximum(np.where(amax > 0, np.frexp(amax)[1] - 1 + 127, 0) - down, 1)
    scale = np.exp2(byte - 127.0)
    codes = (blocks / scale).astype(np.float32).astype(dtype).astype(np.float64)
    return np.moveaxis((codes * scale).reshape(v.shape), -1, axis)


WIDE = False


def mx_kscale(k):
    if not WIDE:
        return np.ones(k)
    levels = np.array([30, -30])
    if k % 512:
        return np.exp2(np.random.permutation(np.resize(levels, k // 32))).repeat(32)
    a = np.empty((k // 512, 16))
    for p in range(k // 512):
        a[p, :8] = np.random.permutation(np.resize(levels, 8))
        for g in range(8):
            far = levels[np.abs(levels - a[p, g]) >= 10]
            a[p, g + 8] = far[np.random.randint(len(far))]
    return np.exp2(a.ravel()).repeat(32)


BF16 = ml_dtypes.bfloat16


def bf(x):
    return np.asarray(x, np.float32).astype(BF16)


def f64(x):
    return np.asarray(x).astype(np.float64)


B, N, T, D, DO, H, E = 128, 2, 8, 512, 512, 8, 128
S = N * T


def sigmoid(v):
    return 1.0 / (1.0 + np.exp(-v))


def setup_inputs():
    r = np.random.standard_normal
    s = mx_kscale(D)
    return {
        "x": bf(r((B, S, D)) * s),
        "edge_features": bf(r((B, E))),
        "Wv": bf(r((D, DO)) / np.sqrt(D) / s[:, None]),
        "bv": bf(r(DO) * 0.3),
        "Wgate": bf(r((E, DO)) / np.sqrt(E)),
        "bgate": bf(r(DO) * 0.3),
        "Wscale": bf(r((E, DO)) * 0.7 / np.sqrt(E)),
        "bscale": bf(r(DO) * 0.3),
        "Wshift": bf(r((E, DO)) * 0.7 / np.sqrt(E)),
        "bshift": bf(r(DO) * 0.3),
    }


def reference(x, edge_features, Wv, bv, Wgate, bgate, Wscale, bscale, Wshift, bshift):
    e = f64(edge_features)
    v = (mxq(f64(x).reshape(B * S, D), 1, "e5m2") @ mxq(f64(Wv), 0, "e5m2")).reshape(B, S, DO) + f64(bv)
    gate = sigmoid(e @ f64(Wgate) + f64(bgate))
    scale = np.tanh(e @ f64(Wscale) + f64(bscale))
    shift = e @ f64(Wshift) + f64(bshift)
    return (v * (1.0 + scale[:, None, :]) + shift[:, None, :]) * gate[:, None, :]

@@ -1,0 +1,200 @@
+from contextlib import ExitStack
+
+import concourse.mybir as mybir
+from concourse.masks import make_identity
+
+B, S, D, DO, E = 128, 16, 512, 512, 128
+FLOPS = 2 * B * S * D * DO + 3 * 2 * B * E * DO
+
+F32 = mybir.dt.float32
+BF16 = mybir.dt.bfloat16
+U32 = mybir.dt.uint32
+U8 = mybir.dt.uint8
+FP8X4 = mybir.dt.float8_e5m2_x4
+ALU = mybir.AluOpType
+ACT = mybir.ActivationFunctionType
+
+P = 128
+PAIR = 2
+NPAIR = S // PAIR
+VEC_ADD = (4, 7, 9, 11, 13, 15)
+X_LOADS = ((0, 1), (1, 2), (2, 4), (4, 8))
+MANUAL = False
+LEAD_T = 3
+LEAD_Q = 2
+LEAD_M = 1
+ACC_BUFS = 4
+XT_BUFS = 3
+
+
+def tile_graphditunit_pa_kernel(
+    tc, x, edge_features, Wv, bv, Wgate, bgate, Wscale, bscale, Wshift, bshift, out
+):
+    nc = tc.nc
+    with ExitStack() as ctx:
+        const = ctx.enter_context(tc.tile_pool(name="const", bufs=1))
+        ps_acc = ctx.enter_context(tc.psum_pool(name="ps_acc", bufs=ACC_BUFS))
+        ps_xt = ctx.enter_context(tc.psum_pool(name="ps_xt", bufs=XT_BUFS))
+        ps_c = ctx.enter_context(tc.psum_pool(name="ps_c", bufs=1))
+        if MANUAL:
+            ctx.enter_context(tc.manual_schedule())
+
+        bias_rows = const.tile([P, DO], BF16, name="bias_rows")
+        nc.gpsimd.memset(bias_rows[:], 0.0)
+        warm_in = const.tile([P, 1], F32, name="warm_in")
+        nc.vector.memset(warm_in[:], 0.0)
+
+        wg_sb = const.tile([P, DO], BF16, name="wg_sb")
+        nc.scalar.dma_start(out=wg_sb[:], in_=Wgate[:, :])
+        ws_sb = const.tile([P, DO], BF16, name="ws_sb")
+        nc.scalar.dma_start(out=ws_sb[:], in_=Wscale[:, :])
+        warm_out = const.tile([P, 1], F32, name="warm_out")
+        nc.scalar.activation(out=warm_out[:], in_=warm_in[:], func=ACT.Sigmoid)
+
+        e_sb = const.tile([P, E], BF16, name="e_sb")
+        nc.sync.dma_start(out=e_sb[:], in_=edge_features[:, :])
+        nc.sync.dma_start(out=bias_rows[0:1, :], in_=bgate.unsqueeze(0))
+        nc.sync.dma_start(out=bias_rows[1:2, :], in_=bscale.unsqueeze(0))
+        w_raw = const.tile([P, 4, DO], BF16, name="w_raw")
+        nc.sync.dma_start(out=w_raw[:], in_=Wv.rearrange("(p j) w -> p j w", j=4))
+        x_of_pair = {}
+        first = True
+        for g0, g1 in X_LOADS:
+            x_t = const.tile([P, PAIR * (g1 - g0), D], BF16, name="x%d" % g0)
+            nc.sync.dma_start(out=x_t[:], in_=x[:, PAIR * g0 : PAIR * g1, :])
+            for g in range(g0, g1):
+                x_of_pair[g] = x_t[:, PAIR * (g - g0) : PAIR * (g - g0 + 1), :]
+            if first:
+                first = False
+                wh_sb = const.tile([P, DO], BF16, name="wh_sb")
+                nc.sync.dma_start(out=wh_sb[:], in_=Wshift[:, :])
+                nc.sync.dma_start(out=bias_rows[2:3, :], in_=bshift.unsqueeze(0))
+                bv_all = const.tile([P, DO], BF16, name="bv_all")
+                nc.sync.dma_start(out=bv_all[:], in_=bv.partition_broadcast(P))
+
+        ident_bf = const.tile([P, P], BF16, name="ident_bf")
+        make_identity(nc, ident_bf[:])
+        ident_f = const.tile([P, P], F32, name="ident_f")
+        make_identity(nc, ident_f[:])
+
+        x_grps = {}
+        x_codes = {}
+        x_scales = {}
+        accs = {}
+
+        def turn(g):
+            words = x_of_pair[g].bitcast(F32)
+            xt = ps_xt.tile([P, PAIR, 2, P], F32, name="xt", tag="xt")
+            for i2 in range(PAIR):
+                for u in range(2):
+                    nc.tensor.transpose(xt[:, i2, u, :], words[:, i2, u : D // 2 : 2], ident_f[:])
+            x_grp = const.tile([P, PAIR * P * 4], BF16, name="x_grp%d" % g, align_bytes=64)
+            nc.scalar.copy(
+                out=x_grp[:].bitcast(F32).rearrange("p (i b u) -> p i b u", i=PAIR, u=2),
+                in_=xt[:].rearrange("p i u b -> p i b u"),
+            )
+            x_grps[g] = x_grp
+
+        def quantise(g):
+            x_codes[g] = const.tile([P, PAIR * P], U32, name="x_codes%d" % g, align_bytes=64)
+            x_scales[g] = const.tile([P, PAIR * P], U8, name="x_scales%d" % g, align_bytes=64)
+            nc.vector.quantize_mx(
+                out=x_codes[g][:].bitcast(FP8X4), scales=x_scales[g][:], in_=x_grps[g][:]
+            )
+
+        def multiply(g):
+            for i2 in range(PAIR):
+                cols = slice(P * i2, P * (i2 + 1))
+                acc = ps_acc.tile([P, DO], F32, name="acc", tag="acc")
+                nc.tensor.matmul_mx(
+                    out=acc[:],
+                    lhsT=x_codes[g][:, cols].bitcast(FP8X4),
+                    lhsT_scale=x_scales[g][:, cols],
+                    rhs=w_codes[:].bitcast(FP8X4),
+                    rhs_scale=w_scales[:],
+                    start=True,
+                    stop=True,
+                )
+                accs[PAIR * g + i2] = acc
+
+        eT_ps = ps_xt.tile([P, P], BF16, name="eT_ps", tag="xt")
+        nc.tensor.transpose(eT_ps[:], e_sb[:], ident_bf[:])
+        eT = const.tile([P, P], BF16, name="eT")
+        nc.vector.tensor_copy(out=eT[:], in_=eT_ps[:])
+
+        zs = []
+        for j, w_sb in enumerate((wg_sb, ws_sb, wh_sb)):
+            z = ps_acc.tile([P, DO], F32, name="z%d" % j, tag="acc")
+            nc.tensor.matmul(
+                out=z[:],
+                lhsT=ident_bf[:, j : j + 1].to_broadcast([P, P]),
+                rhs=bias_rows[:],
+                start=True,
+                stop=False,
+            )
+            nc.tensor.matmul(out=z[:], lhsT=eT[:], rhs=w_sb[:], start=False, stop=True)
+            zs.append(z)
+            if j == 1:
+                turn(0)
+
+        gate = const.tile([P, DO], F32, name="gate")
+        nc.scalar.activation(out=gate[:], in_=zs[0][:], func=ACT.Sigmoid)
+        tanh_s = const.tile([P, DO], F32, name="tanh_s")
+        nc.scalar.activation(out=tanh_s[:], in_=zs[1][:], func=ACT.Tanh)
+
+        w_grp = const.tile([P, DO, 4], BF16, name="w_grp", align_bytes=64)
+        nc.vector.tensor_copy(out=w_grp[:], in_=w_raw[:].rearrange("p j w -> p w j"))
+        w_codes = const.tile([P, DO], U32, name="w_codes", align_bytes=64)
+        w_scales = const.tile([P, DO], U8, name="w_scales", align_bytes=64)
+        nc.vector.quantize_mx(
+            out=w_codes[:].bitcast(FP8X4),
+            scales=w_scales[:],
+            in_=w_grp[:].rearrange("p w j -> p (w j)"),
+        )
+
+        mul_a = const.tile([P, DO], F32, name="mul_a")
+        sh_g = const.tile([P, DO], F32, name="sh_g")
+        bv_a = const.tile([P, DO], F32, name="bv_a")
+        add_c = const.tile([P, DO], F32, name="add_c")
+        c_ps = ps_c.tile([P, DO], F32, name="c_ps")
+
+        quantise(0)
+        nc.vector.scalar_tensor_tensor(
+            out=mul_a[:], in0=tanh_s[:], scalar=1.0, in1=gate[:], op0=ALU.add, op1=ALU.mult
+        )
+        nc.gpsimd.tensor_tensor(out=bv_a[:], in0=bv_all[:], in1=mul_a[:], op=ALU.mult)
+        nc.vector.tensor_tensor(out=sh_g[:], in0=zs[2][:], in1=gate[:], op=ALU.mult)
+        turn(1)
+        multiply(0)
+        quantise(1)
+        turn(2)
+
+        def finish_c():
+            nc.vector.tensor_tensor(out=add_c[:], in0=bv_a[:], in1=sh_g[:], op=ALU.add)
+            ct_ps = ps_xt.tile([P, 4, P], F32, name="ct_ps", tag="xt")
+            for c in range(4):
+                nc.tensor.transpose(ct_ps[:, c, :], add_c[:, P * c : P * (c + 1)], ident_f[:])
+            ct_sb = const.tile([P, 4, P], F32, name="ct_sb")
+            nc.scalar.copy(out=ct_sb[:], in_=ct_ps[:])
+            for c in range(4):
+                nc.tensor.transpose(c_ps[:, P * c : P * (c + 1)], ct_sb[:, c, :], ident_f[:])
+
+        for g in range(NPAIR):
+            if g + LEAD_T < NPAIR:
+                turn(g + LEAD_T)
+            if g + LEAD_Q < NPAIR:
+                quantise(g + LEAD_Q)
+            if g + LEAD_M < NPAIR:
+                multiply(g + LEAD_M)
+            for i2 in range(PAIR):
+                i = PAIR * g + i2
+                prod = const.tile([P, DO], F32, name="prod%d" % i)
+                nc.vector.tensor_tensor(out=prod[:], in0=accs[i][:], in1=mul_a[:], op=ALU.mult)
+                if i == 0:
+                    finish_c()
+                res = const.tile([P, DO], F32, name="res%d" % i)
+                if i in VEC_ADD:
+                    nc.vector.tensor_tensor(out=res[:], in0=prod[:], in1=c_ps[:], op=ALU.add)
+                else:
+                    nc.gpsimd.tensor_tensor(out=res[:], in0=prod[:], in1=add_c[:], op=ALU.add)
+                nc.sync.dma_start(out=out[:, i, :], in_=res[:])

@@ -17,12 +17,13 @@ ACT = mybir.ActivationFunctionType
 P = 128
 PAIR = 2
 NPAIR = S // PAIR
-VEC_ADD = (4, 7, 9, 11, 13, 15)
+NORMAL = 6
+QUAD = 4
+Q0 = PAIR * NORMAL
+VEC_ADD = (5, 10, 11)
 X_LOADS = ((0, 1), (1, 2), (2, 4), (4, 8))
-MANUAL = False
-LEAD_T = 3
-LEAD_Q = 2
-LEAD_M = 1
+TURN_ORDER = (2, 3, 6, 7, 4, 5)
+FIRST_UNIT = 1
 ACC_BUFS = 4
 XT_BUFS = 3
 
@@ -36,8 +37,6 @@ def tile_graphditunit_pa_kernel(
         ps_acc = ctx.enter_context(tc.psum_pool(name="ps_acc", bufs=ACC_BUFS))
         ps_xt = ctx.enter_context(tc.psum_pool(name="ps_xt", bufs=XT_BUFS))
         ps_c = ctx.enter_context(tc.psum_pool(name="ps_c", bufs=1))
-        if MANUAL:
-            ctx.enter_context(tc.manual_schedule())
 
         bias_rows = const.tile([P, DO], BF16, name="bias_rows")
         nc.gpsimd.memset(bias_rows[:], 0.0)
@@ -81,6 +80,9 @@ def tile_graphditunit_pa_kernel(
         x_codes = {}
         x_scales = {}
         accs = {}
+        quad_grp = const.tile([P, QUAD * P * 4], BF16, name="quad_grp", align_bytes=64)
+        quad_codes = const.tile([P, QUAD * P], U32, name="quad_codes", align_bytes=64)
+        quad_scales = const.tile([P, QUAD * P], U8, name="quad_scales", align_bytes=64)
 
         def turn(g):
             words = x_of_pair[g].bitcast(F32)
@@ -88,14 +90,26 @@ def tile_graphditunit_pa_kernel(
             for i2 in range(PAIR):
                 for u in range(2):
                     nc.tensor.transpose(xt[:, i2, u, :], words[:, i2, u : D // 2 : 2], ident_f[:])
-            x_grp = const.tile([P, PAIR * P * 4], BF16, name="x_grp%d" % g, align_bytes=64)
+            if g < NORMAL:
+                x_grp = const.tile([P, PAIR * P * 4], BF16, name="x_grp%d" % g, align_bytes=64)
+                x_grps[g] = x_grp
+                dst = x_grp[:]
+            else:
+                half = PAIR * P * 4
+                dst = quad_grp[:, half * (g - NORMAL) : half * (g - NORMAL + 1)]
             nc.scalar.copy(
-                out=x_grp[:].bitcast(F32).rearrange("p (i b u) -> p i b u", i=PAIR, u=2),
+                out=dst.bitcast(F32).rearrange("p (i b u) -> p i b u", i=PAIR, u=2),
                 in_=xt[:].rearrange("p i u b -> p i b u"),
             )
-            x_grps[g] = x_grp
 
         def quantise(g):
+            if g == NORMAL:
+                return
+            if g == NORMAL + 1:
+                nc.vector.quantize_mx(
+                    out=quad_codes[:].bitcast(FP8X4), scales=quad_scales[:], in_=quad_grp[:]
+                )
+                return
             x_codes[g] = const.tile([P, PAIR * P], U32, name="x_codes%d" % g, align_bytes=64)
             x_scales[g] = const.tile([P, PAIR * P], U8, name="x_scales%d" % g, align_bytes=64)
             nc.vector.quantize_mx(
@@ -156,7 +170,8 @@ def tile_graphditunit_pa_kernel(
         sh_g = const.tile([P, DO], F32, name="sh_g")
         bv_a = const.tile([P, DO], F32, name="bv_a")
         add_c = const.tile([P, DO], F32, name="add_c")
-        c_ps = ps_c.tile([P, DO], F32, name="c_ps")
+        at_sb = const.tile([P, 4, P], F32, name="at_sb")
+        ct_sb = const.tile([P, 4, P], F32, name="ct_sb")
 
         quantise(0)
         nc.vector.scalar_tensor_tensor(
@@ -167,34 +182,85 @@ def tile_graphditunit_pa_kernel(
         turn(1)
         multiply(0)
         quantise(1)
-        turn(2)
+        for g in TURN_ORDER:
+            turn(g)
+            quantise(g)
+
+        def turn_a():
+            at_ps = ps_c.tile([P, 4, P], F32, name="at_ps", tag="c")
+            for c in range(4):
+                nc.tensor.transpose(at_ps[:, c, :], mul_a[:, P * c : P * (c + 1)], ident_f[:])
+            nc.scalar.copy(out=at_sb[:], in_=at_ps[:])
 
         def finish_c():
             nc.vector.tensor_tensor(out=add_c[:], in0=bv_a[:], in1=sh_g[:], op=ALU.add)
-            ct_ps = ps_xt.tile([P, 4, P], F32, name="ct_ps", tag="xt")
+            ct_ps = ps_c.tile([P, 4, P], F32, name="ct_ps", tag="c")
             for c in range(4):
                 nc.tensor.transpose(ct_ps[:, c, :], add_c[:, P * c : P * (c + 1)], ident_f[:])
-            ct_sb = const.tile([P, 4, P], F32, name="ct_sb")
             nc.scalar.copy(out=ct_sb[:], in_=ct_ps[:])
+            c_ps = ps_c.tile([P, DO], F32, name="c_ps", tag="c")
             for c in range(4):
                 nc.tensor.transpose(c_ps[:, P * c : P * (c + 1)], ct_sb[:, c, :], ident_f[:])
+            return c_ps
 
-        for g in range(NPAIR):
-            if g + LEAD_T < NPAIR:
-                turn(g + LEAD_T)
-            if g + LEAD_Q < NPAIR:
-                quantise(g + LEAD_Q)
-            if g + LEAD_M < NPAIR:
-                multiply(g + LEAD_M)
+        acc_ts = {}
+
+        def unit_multiply(u):
+            acc_t = ps_xt.tile([P, QUAD, P], F32, name="acc_t", tag="xt")
+            nc.tensor.matmul_mx(
+                out=acc_t[:].rearrange("p i b -> p (i b)"),
+                lhsT=w_codes[:, P * u : P * (u + 1)].bitcast(FP8X4),
+                lhsT_scale=w_scales[:, P * u : P * (u + 1)],
+                rhs=quad_codes[:].bitcast(FP8X4),
+                rhs_scale=quad_scales[:],
+                start=True,
+                stop=True,
+            )
+            acc_ts[u] = acc_t
+
+        def unit_finish(u):
+            prod_t = const.tile([P, QUAD, P], F32, name="prod_t%d" % u)
+            nc.vector.tensor_tensor(
+                out=prod_t[:],
+                in0=acc_ts[u][:],
+                in1=at_sb[:, u : u + 1, :].to_broadcast([P, QUAD, P]),
+                op=ALU.mult,
+            )
+            back = ps_xt.tile([P, QUAD, P], F32, name="back", tag="xt")
+            for i in range(QUAD):
+                nc.tensor.matmul(
+                    out=back[:, i, :], lhsT=ct_sb[:, u, :], rhs=ident_f[:],
+                    is_transpose=True, start=True, stop=False,
+                )
+                nc.tensor.matmul(
+                    out=back[:, i, :], lhsT=prod_t[:, i, :], rhs=ident_f[:],
+                    is_transpose=True, start=False, stop=True,
+                )
+            res_t = const.tile([P, QUAD, P], F32, name="res_t%d" % u)
+            nc.scalar.copy(out=res_t[:], in_=back[:])
+            nc.scalar.dma_start(out=out[:, Q0 : Q0 + QUAD, P * u : P * (u + 1)], in_=res_t[:])
+
+        turn_a()
+        c_holder = []
+        for g in range(NORMAL):
+            if g + 1 < NORMAL:
+                multiply(g + 1)
+            u = g - FIRST_UNIT
+            if u == -1:
+                unit_multiply(0)
+            if 0 <= u and u + 1 < 4:
+                unit_multiply(u + 1)
+            if 0 <= u and u < 4:
+                unit_finish(u)
             for i2 in range(PAIR):
                 i = PAIR * g + i2
                 prod = const.tile([P, DO], F32, name="prod%d" % i)
                 nc.vector.tensor_tensor(out=prod[:], in0=accs[i][:], in1=mul_a[:], op=ALU.mult)
                 if i == 0:
-                    finish_c()
+                    c_holder.append(finish_c())
                 res = const.tile([P, DO], F32, name="res%d" % i)
                 if i in VEC_ADD:
-                    nc.vector.tensor_tensor(out=res[:], in0=prod[:], in1=c_ps[:], op=ALU.add)
+                    nc.vector.tensor_tensor(out=res[:], in0=prod[:], in1=c_holder[0][:], op=ALU.add)
                 else:
                     nc.gpsimd.tensor_tensor(out=res[:], in0=prod[:], in1=add_c[:], op=ALU.add)
                 nc.sync.dma_start(out=out[:, i, :], in_=res[:])

@@ -40,6 +40,8 @@ def tile_graphditunit_pa_kernel(
 
         bias_rows = const.tile([P, DO], BF16, name="bias_rows")
         nc.gpsimd.memset(bias_rows[:], 0.0)
+        late_rows = const.tile([P, DO], BF16, name="late_rows")
+        nc.vector.memset(late_rows[:], 0.0)
         warm_in = const.tile([P, 1], F32, name="warm_in")
         nc.vector.memset(warm_in[:], 0.0)
 
@@ -67,9 +69,8 @@ def tile_graphditunit_pa_kernel(
                 first = False
                 wh_sb = const.tile([P, DO], BF16, name="wh_sb")
                 nc.sync.dma_start(out=wh_sb[:], in_=Wshift[:, :])
-                nc.sync.dma_start(out=bias_rows[2:3, :], in_=bshift.unsqueeze(0))
-                bv_all = const.tile([P, DO], BF16, name="bv_all")
-                nc.sync.dma_start(out=bv_all[:], in_=bv.partition_broadcast(P))
+                nc.sync.dma_start(out=late_rows[0:1, :], in_=bshift.unsqueeze(0))
+                nc.sync.dma_start(out=late_rows[1:2, :], in_=bv.unsqueeze(0))
 
         ident_bf = const.tile([P, P], BF16, name="ident_bf")
         make_identity(nc, ident_bf[:])
@@ -141,8 +142,8 @@ def tile_graphditunit_pa_kernel(
             z = ps_acc.tile([P, DO], F32, name="z%d" % j, tag="acc")
             nc.tensor.matmul(
                 out=z[:],
-                lhsT=ident_bf[:, j : j + 1].to_broadcast([P, P]),
-                rhs=bias_rows[:],
+                lhsT=ident_bf[:, j % 2 : j % 2 + 1].to_broadcast([P, P]),
+                rhs=(bias_rows if j < 2 else late_rows)[:],
                 start=True,
                 stop=False,
             )
@@ -150,6 +151,19 @@ def tile_graphditunit_pa_kernel(
             zs.append(z)
             if j == 1:
                 turn(0)
+
+        rows_t = ps_c.tile([P, 4, P], BF16, name="rows_t", tag="c")
+        for c in range(4):
+            nc.tensor.transpose(rows_t[:, c, :], late_rows[:, P * c : P * (c + 1)], ident_bf[:])
+        bv_col = const.tile([P, 4], BF16, name="bv_col")
+        nc.scalar.copy(out=bv_col[:], in_=rows_t[:, :, 1])
+        bv_ps = ps_c.tile([P, DO], BF16, name="bv_ps", tag="c")
+        for c in range(4):
+            nc.tensor.transpose(
+                bv_ps[:, P * c : P * (c + 1)], bv_col[:, c : c + 1].to_broadcast([P, P]), ident_bf[:]
+            )
+        bv_all = const.tile([P, DO], BF16, name="bv_all")
+        nc.scalar.copy(out=bv_all[:], in_=bv_ps[:])
 
         gate = const.tile([P, DO], F32, name="gate")
         nc.scalar.activation(out=gate[:], in_=zs[0][:], func=ACT.Sigmoid)

@@ -170,15 +170,33 @@ def tile_graphditunit_pa_kernel(
         tanh_s = const.tile([P, DO], F32, name="tanh_s")
         nc.scalar.activation(out=tanh_s[:], in_=zs[1][:], func=ACT.Tanh)
 
-        w_grp = const.tile([P, DO, 4], BF16, name="w_grp", align_bytes=64)
-        nc.vector.tensor_copy(out=w_grp[:], in_=w_raw[:].rearrange("p j w -> p w j"))
+        HALF = DO // 2
+        QUARTER = DO // 4
         w_codes = const.tile([P, DO], U32, name="w_codes", align_bytes=64)
         w_scales = const.tile([P, DO], U8, name="w_scales", align_bytes=64)
-        nc.vector.quantize_mx(
-            out=w_codes[:].bitcast(FP8X4),
-            scales=w_scales[:],
-            in_=w_grp[:].rearrange("p w j -> p (w j)"),
+        w_grps = []
+        for h in range(2):
+            w_grp = const.tile([P, HALF, 4], BF16, name="w_grp%d" % h, align_bytes=64)
+            w_grps.append(w_grp)
+        nc.vector.tensor_copy(out=w_grps[0][:], in_=w_raw[:, :, 0:HALF].rearrange("p j w -> p w j"))
+        nc.scalar.copy(
+            out=w_grps[1][:, 0:QUARTER, :],
+            in_=w_raw[:, :, HALF : HALF + QUARTER].rearrange("p j w -> p w j"),
         )
+        nc.gpsimd.tensor_scalar(
+            out=w_grps[1][:, QUARTER:HALF, :],
+            in0=w_raw[:, :, HALF + QUARTER : DO].rearrange("p j w -> p w j"),
+            scalar1=1.0,
+            scalar2=0.0,
+            op0=ALU.mult,
+            op1=ALU.add,
+        )
+        for h in range(2):
+            nc.vector.quantize_mx(
+                out=w_codes[:, HALF * h : HALF * (h + 1)].bitcast(FP8X4),
+                scales=w_scales[:, HALF * h : HALF * (h + 1)],
+                in_=w_grps[h][:].rearrange("p w j -> p (w j)"),
+            )
 
         mul_a = const.tile([P, DO], F32, name="mul_a")
         sh_g = const.tile([P, DO], F32, name="sh_g")
@@ -273,6 +291,14 @@ def tile_graphditunit_pa_kernel(
                 if i == 0:
                     c_holder.append(finish_c())
                 res = const.tile([P, DO], F32, name="res%d" % i)
+                if i == PAIR * NORMAL - 1:
+                    for h in range(2):
+                        cols = slice(DO // 2 * h, DO // 2 * (h + 1))
+                        nc.vector.tensor_tensor(
+                            out=res[:, cols], in0=prod[:, cols], in1=c_holder[0][:, cols], op=ALU.add
+                        )
+                        nc.sync.dma_start(out=out[:, i, cols], in_=res[:, cols])
+                    continue
                 if i in VEC_ADD:
                     nc.vector.tensor_tensor(out=res[:], in0=prod[:], in1=c_holder[0][:], op=ALU.add)
                 else:

@@ -20,7 +20,8 @@ NPAIR = S // PAIR
 NORMAL = 6
 QUAD = 4
 Q0 = PAIR * NORMAL
-VEC_ADD = (5, 10, 11)
+VEC_ADD = (5, 8, 10, 11)
+ROW_OF = (0, 32, 0)
 X_LOADS = ((0, 1), (1, 2), (2, 4), (4, 8))
 TURN_ORDER = (2, 3, 6, 7, 4, 5)
 FIRST_UNIT = 1
@@ -54,8 +55,11 @@ def tile_graphditunit_pa_kernel(
 
         e_sb = const.tile([P, E], BF16, name="e_sb")
         nc.sync.dma_start(out=e_sb[:], in_=edge_features[:, :])
-        nc.sync.dma_start(out=bias_rows[0:1, :], in_=bgate.unsqueeze(0))
-        nc.sync.dma_start(out=bias_rows[1:2, :], in_=bscale.unsqueeze(0))
+        stage_rows = const.tile([P, DO], BF16, name="stage_rows")
+        nc.sync.dma_start(out=stage_rows[0:1, :], in_=bgate.unsqueeze(0))
+        nc.sync.dma_start(out=stage_rows[32:33, :], in_=bscale.unsqueeze(0))
+        nc.scalar.copy(out=bias_rows[0:1, :], in_=stage_rows[0:1, :])
+        nc.scalar.copy(out=bias_rows[32:33, :], in_=stage_rows[32:33, :])
         w_raw = const.tile([P, 4, DO], BF16, name="w_raw")
         nc.sync.dma_start(out=w_raw[:], in_=Wv.rearrange("(p j) w -> p j w", j=4))
         x_of_pair = {}
@@ -135,14 +139,14 @@ def tile_graphditunit_pa_kernel(
         eT_ps = ps_xt.tile([P, P], BF16, name="eT_ps", tag="xt")
         nc.tensor.transpose(eT_ps[:], e_sb[:], ident_bf[:])
         eT = const.tile([P, P], BF16, name="eT")
-        nc.vector.tensor_copy(out=eT[:], in_=eT_ps[:])
+        nc.scalar.copy(out=eT[:], in_=eT_ps[:])
 
         zs = []
         for j, w_sb in enumerate((wg_sb, ws_sb, wh_sb)):
             z = ps_acc.tile([P, DO], F32, name="z%d" % j, tag="acc")
             nc.tensor.matmul(
                 out=z[:],
-                lhsT=ident_bf[:, j % 2 : j % 2 + 1].to_broadcast([P, P]),
+                lhsT=ident_bf[:, ROW_OF[j] : ROW_OF[j] + 1].to_broadcast([P, P]),
                 rhs=(bias_rows if j < 2 else late_rows)[:],
                 start=True,
                 stop=False,
@@ -171,7 +175,7 @@ def tile_graphditunit_pa_kernel(
         nc.scalar.activation(out=tanh_s[:], in_=zs[1][:], func=ACT.Tanh)
 
         HALF = DO // 2
-        QUARTER = DO // 4
+        QUARTER = 160
         w_codes = const.tile([P, DO], U32, name="w_codes", align_bytes=64)
         w_scales = const.tile([P, DO], U8, name="w_scales", align_bytes=64)
         w_grps = []
@@ -225,7 +229,7 @@ def tile_graphditunit_pa_kernel(
             nc.scalar.copy(out=at_sb[:], in_=at_ps[:])
 
         def finish_c():
-            nc.vector.tensor_tensor(out=add_c[:], in0=bv_a[:], in1=sh_g[:], op=ALU.add)
+            nc.gpsimd.tensor_tensor(out=add_c[:], in0=bv_a[:], in1=sh_g[:], op=ALU.add)
             ct_ps = ps_c.tile([P, 4, P], F32, name="ct_ps", tag="c")
             for c in range(4):
                 nc.tensor.transpose(ct_ps[:, c, :], add_c[:, P * c : P * (c + 1)], ident_f[:])

@@ -39,8 +39,10 @@ def tile_graphditunit_pa_kernel(
         ps_xt = ctx.enter_context(tc.psum_pool(name="ps_xt", bufs=XT_BUFS))
         ps_c = ctx.enter_context(tc.psum_pool(name="ps_c", bufs=1))
 
-        bias_rows = const.tile([P, DO], BF16, name="bias_rows")
-        nc.gpsimd.memset(bias_rows[:], 0.0)
+        bias_g = const.tile([P, DO], BF16, name="bias_g")
+        nc.gpsimd.memset(bias_g[:], 0.0)
+        bias_s = const.tile([P, DO], BF16, name="bias_s")
+        nc.vector.memset(bias_s[:], 0.0)
         late_rows = const.tile([P, DO], BF16, name="late_rows")
         nc.vector.memset(late_rows[:], 0.0)
         warm_in = const.tile([P, 1], F32, name="warm_in")
@@ -53,13 +55,15 @@ def tile_graphditunit_pa_kernel(
         warm_out = const.tile([P, 1], F32, name="warm_out")
         nc.scalar.activation(out=warm_out[:], in_=warm_in[:], func=ACT.Sigmoid)
 
-        e_sb = const.tile([P, E], BF16, name="e_sb")
-        nc.sync.dma_start(out=e_sb[:], in_=edge_features[:, :])
         stage_rows = const.tile([P, DO], BF16, name="stage_rows")
         nc.sync.dma_start(out=stage_rows[0:1, :], in_=bgate.unsqueeze(0))
         nc.sync.dma_start(out=stage_rows[32:33, :], in_=bscale.unsqueeze(0))
-        nc.scalar.copy(out=bias_rows[0:1, :], in_=stage_rows[0:1, :])
-        nc.scalar.copy(out=bias_rows[32:33, :], in_=stage_rows[32:33, :])
+        e_sb = const.tile([P, E], BF16, name="e_sb")
+        nc.sync.dma_start(out=e_sb[:], in_=edge_features[:, :])
+        bv_c = const.tile([P, 4], BF16, name="bv_c")
+        nc.sync.dma_start(out=bv_c[:], in_=bv.rearrange("(p c) -> p c", c=4))
+        nc.vector.tensor_copy(out=bias_g[0:1, :], in_=stage_rows[0:1, :])
+        nc.vector.tensor_copy(out=bias_s[32:33, :], in_=stage_rows[32:33, :])
         w_raw = const.tile([P, 4, DO], BF16, name="w_raw")
         nc.sync.dma_start(out=w_raw[:], in_=Wv.rearrange("(p j) w -> p j w", j=4))
         x_of_pair = {}
@@ -74,7 +78,6 @@ def tile_graphditunit_pa_kernel(
                 wh_sb = const.tile([P, DO], BF16, name="wh_sb")
                 nc.sync.dma_start(out=wh_sb[:], in_=Wshift[:, :])
                 nc.sync.dma_start(out=late_rows[0:1, :], in_=bshift.unsqueeze(0))
-                nc.sync.dma_start(out=late_rows[1:2, :], in_=bv.unsqueeze(0))
 
         ident_bf = const.tile([P, P], BF16, name="ident_bf")
         make_identity(nc, ident_bf[:])
@@ -136,38 +139,35 @@ def tile_graphditunit_pa_kernel(
                 )
                 accs[PAIR * g + i2] = acc
 
+        zs = []
+        for j, rows in enumerate((bias_g, bias_s, late_rows)):
+            z = ps_acc.tile([P, DO], F32, name="z%d" % j, tag="acc")
+            zs.append(z)
+            if j < 2:
+                nc.tensor.matmul(
+                    out=z[:], lhsT=ident_bf[:, ROW_OF[j] : ROW_OF[j] + 1].to_broadcast([P, P]), rhs=rows[:],
+                    start=True, stop=False,
+                )
         eT_ps = ps_xt.tile([P, P], BF16, name="eT_ps", tag="xt")
         nc.tensor.transpose(eT_ps[:], e_sb[:], ident_bf[:])
         eT = const.tile([P, P], BF16, name="eT")
         nc.scalar.copy(out=eT[:], in_=eT_ps[:])
+        nc.tensor.matmul(out=zs[0][:], lhsT=eT[:], rhs=wg_sb[:], start=False, stop=True)
+        nc.tensor.matmul(out=zs[1][:], lhsT=eT[:], rhs=ws_sb[:], start=False, stop=True)
+        turn(0)
+        nc.tensor.matmul(
+            out=zs[2][:], lhsT=ident_bf[:, ROW_OF[2] : ROW_OF[2] + 1].to_broadcast([P, P]), rhs=late_rows[:],
+            start=True, stop=False,
+        )
+        nc.tensor.matmul(out=zs[2][:], lhsT=eT[:], rhs=wh_sb[:], start=False, stop=True)
 
-        zs = []
-        for j, w_sb in enumerate((wg_sb, ws_sb, wh_sb)):
-            z = ps_acc.tile([P, DO], F32, name="z%d" % j, tag="acc")
-            nc.tensor.matmul(
-                out=z[:],
-                lhsT=ident_bf[:, ROW_OF[j] : ROW_OF[j] + 1].to_broadcast([P, P]),
-                rhs=(bias_rows if j < 2 else late_rows)[:],
-                start=True,
-                stop=False,
-            )
-            nc.tensor.matmul(out=z[:], lhsT=eT[:], rhs=w_sb[:], start=False, stop=True)
-            zs.append(z)
-            if j == 1:
-                turn(0)
-
-        rows_t = ps_c.tile([P, 4, P], BF16, name="rows_t", tag="c")
+        bv_ps = ps_c.tile([P, 4, P], BF16, name="bv_ps", tag="c")
         for c in range(4):
-            nc.tensor.transpose(rows_t[:, c, :], late_rows[:, P * c : P * (c + 1)], ident_bf[:])
-        bv_col = const.tile([P, 4], BF16, name="bv_col")
-        nc.scalar.copy(out=bv_col[:], in_=rows_t[:, :, 1])
-        bv_ps = ps_c.tile([P, DO], BF16, name="bv_ps", tag="c")
-        for c in range(4):
-            nc.tensor.transpose(
-                bv_ps[:, P * c : P * (c + 1)], bv_col[:, c : c + 1].to_broadcast([P, P]), ident_bf[:]
-            )
+            nc.tensor.transpose(bv_ps[:, c, :], bv_c[:, c : c + 1].to_broadcast([P, P]), ident_bf[:])
         bv_all = const.tile([P, DO], BF16, name="bv_all")
-        nc.scalar.copy(out=bv_all[:], in_=bv_ps[:])
+        nc.vector.tensor_copy(
+            out=bv_all[:].rearrange("p (n c) -> p n c", c=4), in_=bv_ps[:].rearrange("p c n -> p n c")
+        )
 
         gate = const.tile([P, DO], F32, name="gate")
         nc.scalar.activation(out=gate[:], in_=zs[0][:], func=ACT.Sigmoid)

@@ -20,7 +20,7 @@ NPAIR = S // PAIR
 NORMAL = 6
 QUAD = 4
 Q0 = PAIR * NORMAL
-VEC_ADD = (5, 8, 10, 11)
+VEC_ADD = (3, 5, 7, 9, 10, 11)
 ROW_OF = (0, 32, 0)
 X_LOADS = ((0, 1), (1, 2), (2, 4), (4, 8))
 TURN_ORDER = (2, 3, 6, 7, 4, 5)

@@ -20,7 +20,7 @@ NPAIR = S // PAIR
 NORMAL = 6
 QUAD = 4
 Q0 = PAIR * NORMAL
-VEC_ADD = (3, 5, 7, 9, 10, 11)
+VEC_ADD = (5, 7, 9, 10, 11)
 ROW_OF = (0, 32, 0)
 X_LOADS = ((0, 1), (1, 2), (2, 4), (4, 8))
 TURN_ORDER = (2, 3, 6, 7, 4, 5)
@@ -55,13 +55,13 @@ def tile_graphditunit_pa_kernel(
         warm_out = const.tile([P, 1], F32, name="warm_out")
         nc.scalar.activation(out=warm_out[:], in_=warm_in[:], func=ACT.Sigmoid)
 
+        bv_c = const.tile([P, 4], BF16, name="bv_c")
+        nc.sync.dma_start(out=bv_c[:], in_=bv.rearrange("(p c) -> p c", c=4))
         stage_rows = const.tile([P, DO], BF16, name="stage_rows")
         nc.sync.dma_start(out=stage_rows[0:1, :], in_=bgate.unsqueeze(0))
         nc.sync.dma_start(out=stage_rows[32:33, :], in_=bscale.unsqueeze(0))
         e_sb = const.tile([P, E], BF16, name="e_sb")
         nc.sync.dma_start(out=e_sb[:], in_=edge_features[:, :])
-        bv_c = const.tile([P, 4], BF16, name="bv_c")
-        nc.sync.dma_start(out=bv_c[:], in_=bv.rearrange("(p c) -> p c", c=4))
         nc.vector.tensor_copy(out=bias_g[0:1, :], in_=stage_rows[0:1, :])
         nc.vector.tensor_copy(out=bias_s[32:33, :], in_=stage_rows[32:33, :])
         w_raw = const.tile([P, 4, DO], BF16, name="w_raw")
@@ -139,6 +139,14 @@ def tile_graphditunit_pa_kernel(
                 )
                 accs[PAIR * g + i2] = acc
 
+        bv_ps = ps_c.tile([P, 4, P], BF16, name="bv_ps", tag="c")
+        for c in range(4):
+            nc.tensor.transpose(bv_ps[:, c, :], bv_c[:, c : c + 1].to_broadcast([P, P]), ident_bf[:])
+        bv_all = const.tile([P, DO], BF16, name="bv_all")
+        nc.vector.tensor_copy(
+            out=bv_all[:].rearrange("p (n c) -> p n c", c=4), in_=bv_ps[:].rearrange("p c n -> p n c")
+        )
+
         zs = []
         for j, rows in enumerate((bias_g, bias_s, late_rows)):
             z = ps_acc.tile([P, DO], F32, name="z%d" % j, tag="acc")
@@ -160,14 +168,6 @@ def tile_graphditunit_pa_kernel(
             start=True, stop=False,
         )
         nc.tensor.matmul(out=zs[2][:], lhsT=eT[:], rhs=wh_sb[:], start=False, stop=True)
-
-        bv_ps = ps_c.tile([P, 4, P], BF16, name="bv_ps", tag="c")
-        for c in range(4):
-            nc.tensor.transpose(bv_ps[:, c, :], bv_c[:, c : c + 1].to_broadcast([P, P]), ident_bf[:])
-        bv_all = const.tile([P, DO], BF16, name="bv_all")
-        nc.vector.tensor_copy(
-            out=bv_all[:].rearrange("p (n c) -> p n c", c=4), in_=bv_ps[:].rearrange("p c n -> p n c")
-        )
 
         gate = const.tile([P, DO], F32, name="gate")
         nc.scalar.activation(out=gate[:], in_=zs[0][:], func=ACT.Sigmoid)

@@ -22,7 +22,7 @@ QUAD = 4
 Q0 = PAIR * NORMAL
 VEC_ADD = (5, 7, 9, 10, 11)
 ROW_OF = (0, 32, 0)
-X_LOADS = ((0, 1), (1, 2), (2, 4), (4, 8))
+X_LOADS = ((0, 1), (1, 2), (2, 4), (6, 8), (4, 6))
 TURN_ORDER = (2, 3, 6, 7, 4, 5)
 FIRST_UNIT = 1
 ACC_BUFS = 4

@@ -21,7 +21,7 @@ NORMAL = 6
 QUAD = 4
 Q0 = PAIR * NORMAL
 VEC_ADD = (5, 7, 9, 10, 11)
-ROW_OF = (0, 32, 0)
+ROW_OF = (0, 32, 64)
 X_LOADS = ((0, 1), (1, 2), (2, 4), (6, 8), (4, 6))
 TURN_ORDER = (2, 3, 6, 7, 4, 5)
 FIRST_UNIT = 1
@@ -62,8 +62,10 @@ def tile_graphditunit_pa_kernel(
         nc.sync.dma_start(out=stage_rows[32:33, :], in_=bscale.unsqueeze(0))
         e_sb = const.tile([P, E], BF16, name="e_sb")
         nc.sync.dma_start(out=e_sb[:], in_=edge_features[:, :])
+        nc.sync.dma_start(out=stage_rows[64:65, :], in_=bshift.unsqueeze(0))
         nc.vector.tensor_copy(out=bias_g[0:1, :], in_=stage_rows[0:1, :])
         nc.vector.tensor_copy(out=bias_s[32:33, :], in_=stage_rows[32:33, :])
+        nc.vector.tensor_copy(out=late_rows[64:65, :], in_=stage_rows[64:65, :])
         w_raw = const.tile([P, 4, DO], BF16, name="w_raw")
         nc.sync.dma_start(out=w_raw[:], in_=Wv.rearrange("(p j) w -> p j w", j=4))
         x_of_pair = {}
@@ -77,7 +79,6 @@ def tile_graphditunit_pa_kernel(
                 first = False
                 wh_sb = const.tile([P, DO], BF16, name="wh_sb")
                 nc.sync.dma_start(out=wh_sb[:], in_=Wshift[:, :])
-                nc.sync.dma_start(out=late_rows[0:1, :], in_=bshift.unsqueeze(0))
 
         ident_bf = const.tile([P, P], BF16, name="ident_bf")
         make_identity(nc, ident_bf[:])
@@ -160,13 +161,13 @@ def tile_graphditunit_pa_kernel(
         nc.tensor.transpose(eT_ps[:], e_sb[:], ident_bf[:])
         eT = const.tile([P, P], BF16, name="eT")
         nc.scalar.copy(out=eT[:], in_=eT_ps[:])
-        nc.tensor.matmul(out=zs[0][:], lhsT=eT[:], rhs=wg_sb[:], start=False, stop=True)
-        nc.tensor.matmul(out=zs[1][:], lhsT=eT[:], rhs=ws_sb[:], start=False, stop=True)
-        turn(0)
         nc.tensor.matmul(
             out=zs[2][:], lhsT=ident_bf[:, ROW_OF[2] : ROW_OF[2] + 1].to_broadcast([P, P]), rhs=late_rows[:],
             start=True, stop=False,
         )
+        nc.tensor.matmul(out=zs[0][:], lhsT=eT[:], rhs=wg_sb[:], start=False, stop=True)
+        nc.tensor.matmul(out=zs[1][:], lhsT=eT[:], rhs=ws_sb[:], start=False, stop=True)
+        turn(0)
         nc.tensor.matmul(out=zs[2][:], lhsT=eT[:], rhs=wh_sb[:], start=False, stop=True)
 
         gate = const.tile([P, DO], F32, name="gate")

from contextlib import ExitStack

import concourse.mybir as mybir
from concourse.masks import make_identity

B, S, D, DO, E = 128, 16, 512, 512, 128
FLOPS = 2 * B * S * D * DO + 3 * 2 * B * E * DO

F32 = mybir.dt.float32
BF16 = mybir.dt.bfloat16
U32 = mybir.dt.uint32
U8 = mybir.dt.uint8
FP8X4 = mybir.dt.float8_e5m2_x4
ALU = mybir.AluOpType
ACT = mybir.ActivationFunctionType

P = 128
PAIR = 2
NPAIR = S // PAIR
NORMAL = 6
QUAD = 4
Q0 = PAIR * NORMAL
VEC_ADD = (5, 7, 9, 10, 11)
ROW_OF = (0, 32, 64)
X_LOADS = ((0, 1), (1, 2), (2, 4), (6, 8), (4, 6))
TURN_ORDER = (2, 3, 6, 7, 4, 5)
FIRST_UNIT = 1
ACC_BUFS = 4
XT_BUFS = 3


def tile_graphditunit_pa_kernel(
    tc, x, edge_features, Wv, bv, Wgate, bgate, Wscale, bscale, Wshift, bshift, out
):
    nc = tc.nc
    with ExitStack() as ctx:
        const = ctx.enter_context(tc.tile_pool(name="const", bufs=1))
        ps_acc = ctx.enter_context(tc.psum_pool(name="ps_acc", bufs=ACC_BUFS))
        ps_xt = ctx.enter_context(tc.psum_pool(name="ps_xt", bufs=XT_BUFS))
        ps_c = ctx.enter_context(tc.psum_pool(name="ps_c", bufs=1))

        bias_g = const.tile([P, DO], BF16, name="bias_g")
        nc.gpsimd.memset(bias_g[:], 0.0)
        bias_s = const.tile([P, DO], BF16, name="bias_s")
        nc.vector.memset(bias_s[:], 0.0)
        late_rows = const.tile([P, DO], BF16, name="late_rows")
        nc.vector.memset(late_rows[:], 0.0)
        warm_in = const.tile([P, 1], F32, name="warm_in")
        nc.vector.memset(warm_in[:], 0.0)

        wg_sb = const.tile([P, DO], BF16, name="wg_sb")
        nc.scalar.dma_start(out=wg_sb[:], in_=Wgate[:, :])
        ws_sb = const.tile([P, DO], BF16, name="ws_sb")
        nc.scalar.dma_start(out=ws_sb[:], in_=Wscale[:, :])
        warm_out = const.tile([P, 1], F32, name="warm_out")
        nc.scalar.activation(out=warm_out[:], in_=warm_in[:], func=ACT.Sigmoid)

        bv_c = const.tile([P, 4], BF16, name="bv_c")
        nc.sync.dma_start(out=bv_c[:], in_=bv.rearrange("(p c) -> p c", c=4))
        stage_rows = const.tile([P, DO], BF16, name="stage_rows")
        nc.sync.dma_start(out=stage_rows[0:1, :], in_=bgate.unsqueeze(0))
        nc.sync.dma_start(out=stage_rows[32:33, :], in_=bscale.unsqueeze(0))
        e_sb = const.tile([P, E], BF16, name="e_sb")
        nc.sync.dma_start(out=e_sb[:], in_=edge_features[:, :])
        nc.sync.dma_start(out=stage_rows[64:65, :], in_=bshift.unsqueeze(0))
        nc.vector.tensor_copy(out=bias_g[0:1, :], in_=stage_rows[0:1, :])
        nc.vector.tensor_copy(out=bias_s[32:33, :], in_=stage_rows[32:33, :])
        nc.vector.tensor_copy(out=late_rows[64:65, :], in_=stage_rows[64:65, :])
        w_raw = const.tile([P, 4, DO], BF16, name="w_raw")
        nc.sync.dma_start(out=w_raw[:], in_=Wv.rearrange("(p j) w -> p j w", j=4))
        x_of_pair = {}
        first = True
        for g0, g1 in X_LOADS:
            x_t = const.tile([P, PAIR * (g1 - g0), D], BF16, name="x%d" % g0)
            nc.sync.dma_start(out=x_t[:], in_=x[:, PAIR * g0 : PAIR * g1, :])
            for g in range(g0, g1):
                x_of_pair[g] = x_t[:, PAIR * (g - g0) : PAIR * (g - g0 + 1), :]
            if first:
                first = False
                wh_sb = const.tile([P, DO], BF16, name="wh_sb")
                nc.sync.dma_start(out=wh_sb[:], in_=Wshift[:, :])

        ident_bf = const.tile([P, P], BF16, name="ident_bf")
        make_identity(nc, ident_bf[:])
        ident_f = const.tile([P, P], F32, name="ident_f")
        make_identity(nc, ident_f[:])

        x_grps = {}
        x_codes = {}
        x_scales = {}
        accs = {}
        quad_grp = const.tile([P, QUAD * P * 4], BF16, name="quad_grp", align_bytes=64)
        quad_codes = const.tile([P, QUAD * P], U32, name="quad_codes", align_bytes=64)
        quad_scales = const.tile([P, QUAD * P], U8, name="quad_scales", align_bytes=64)

        def turn(g):
            words = x_of_pair[g].bitcast(F32)
            xt = ps_xt.tile([P, PAIR, 2, P], F32, name="xt", tag="xt")
            for i2 in range(PAIR):
                for u in range(2):
                    nc.tensor.transpose(xt[:, i2, u, :], words[:, i2, u : D // 2 : 2], ident_f[:])
            if g < NORMAL:
                x_grp = const.tile([P, PAIR * P * 4], BF16, name="x_grp%d" % g, align_bytes=64)
                x_grps[g] = x_grp
                dst = x_grp[:]
            else:
                half = PAIR * P * 4
                dst = quad_grp[:, half * (g - NORMAL) : half * (g - NORMAL + 1)]
            nc.scalar.copy(
                out=dst.bitcast(F32).rearrange("p (i b u) -> p i b u", i=PAIR, u=2),
                in_=xt[:].rearrange("p i u b -> p i b u"),
            )

        def quantise(g):
            if g == NORMAL:
                return
            if g == NORMAL + 1:
                nc.vector.quantize_mx(
                    out=quad_codes[:].bitcast(FP8X4), scales=quad_scales[:], in_=quad_grp[:]
                )
                return
            x_codes[g] = const.tile([P, PAIR * P], U32, name="x_codes%d" % g, align_bytes=64)
            x_scales[g] = const.tile([P, PAIR * P], U8, name="x_scales%d" % g, align_bytes=64)
            nc.vector.quantize_mx(
                out=x_codes[g][:].bitcast(FP8X4), scales=x_scales[g][:], in_=x_grps[g][:]
            )

        def multiply(g):
            for i2 in range(PAIR):
                cols = slice(P * i2, P * (i2 + 1))
                acc = ps_acc.tile([P, DO], F32, name="acc", tag="acc")
                nc.tensor.matmul_mx(
                    out=acc[:],
                    lhsT=x_codes[g][:, cols].bitcast(FP8X4),
                    lhsT_scale=x_scales[g][:, cols],
                    rhs=w_codes[:].bitcast(FP8X4),
                    rhs_scale=w_scales[:],
                    start=True,
                    stop=True,
                )
                accs[PAIR * g + i2] = acc

        bv_ps = ps_c.tile([P, 4, P], BF16, name="bv_ps", tag="c")
        for c in range(4):
            nc.tensor.transpose(bv_ps[:, c, :], bv_c[:, c : c + 1].to_broadcast([P, P]), ident_bf[:])
        bv_all = const.tile([P, DO], BF16, name="bv_all")
        nc.vector.tensor_copy(
            out=bv_all[:].rearrange("p (n c) -> p n c", c=4), in_=bv_ps[:].rearrange("p c n -> p n c")
        )

        zs = []
        for j, rows in enumerate((bias_g, bias_s, late_rows)):
            z = ps_acc.tile([P, DO], F32, name="z%d" % j, tag="acc")
            zs.append(z)
            if j < 2:
                nc.tensor.matmul(
                    out=z[:], lhsT=ident_bf[:, ROW_OF[j] : ROW_OF[j] + 1].to_broadcast([P, P]), rhs=rows[:],
                    start=True, stop=False,
                )
        eT_ps = ps_xt.tile([P, P], BF16, name="eT_ps", tag="xt")
        nc.tensor.transpose(eT_ps[:], e_sb[:], ident_bf[:])
        eT = const.tile([P, P], BF16, name="eT")
        nc.scalar.copy(out=eT[:], in_=eT_ps[:])
        nc.tensor.matmul(
            out=zs[2][:], lhsT=ident_bf[:, ROW_OF[2] : ROW_OF[2] + 1].to_broadcast([P, P]), rhs=late_rows[:],
            start=True, stop=False,
        )
        nc.tensor.matmul(out=zs[0][:], lhsT=eT[:], rhs=wg_sb[:], start=False, stop=True)
        nc.tensor.matmul(out=zs[1][:], lhsT=eT[:], rhs=ws_sb[:], start=False, stop=True)
        turn(0)
        nc.tensor.matmul(out=zs[2][:], lhsT=eT[:], rhs=wh_sb[:], start=False, stop=True)

        gate = const.tile([P, DO], F32, name="gate")
        nc.scalar.activation(out=gate[:], in_=zs[0][:], func=ACT.Sigmoid)
        tanh_s = const.tile([P, DO], F32, name="tanh_s")
        nc.scalar.activation(out=tanh_s[:], in_=zs[1][:], func=ACT.Tanh)

        HALF = DO // 2
        QUARTER = 160
        w_codes = const.tile([P, DO], U32, name="w_codes", align_bytes=64)
        w_scales = const.tile([P, DO], U8, name="w_scales", align_bytes=64)
        w_grps = []
        for h in range(2):
            w_grp = const.tile([P, HALF, 4], BF16, name="w_grp%d" % h, align_bytes=64)
            w_grps.append(w_grp)
        nc.vector.tensor_copy(out=w_grps[0][:], in_=w_raw[:, :, 0:HALF].rearrange("p j w -> p w j"))
        nc.scalar.copy(
            out=w_grps[1][:, 0:QUARTER, :],
            in_=w_raw[:, :, HALF : HALF + QUARTER].rearrange("p j w -> p w j"),
        )
        nc.gpsimd.tensor_scalar(
            out=w_grps[1][:, QUARTER:HALF, :],
            in0=w_raw[:, :, HALF + QUARTER : DO].rearrange("p j w -> p w j"),
            scalar1=1.0,
            scalar2=0.0,
            op0=ALU.mult,
            op1=ALU.add,
        )
        for h in range(2):
            nc.vector.quantize_mx(
                out=w_codes[:, HALF * h : HALF * (h + 1)].bitcast(FP8X4),
                scales=w_scales[:, HALF * h : HALF * (h + 1)],
                in_=w_grps[h][:].rearrange("p w j -> p (w j)"),
            )

        mul_a = const.tile([P, DO], F32, name="mul_a")
        sh_g = const.tile([P, DO], F32, name="sh_g")
        bv_a = const.tile([P, DO], F32, name="bv_a")
        add_c = const.tile([P, DO], F32, name="add_c")
        at_sb = const.tile([P, 4, P], F32, name="at_sb")
        ct_sb = const.tile([P, 4, P], F32, name="ct_sb")

        quantise(0)
        nc.vector.scalar_tensor_tensor(
            out=mul_a[:], in0=tanh_s[:], scalar=1.0, in1=gate[:], op0=ALU.add, op1=ALU.mult
        )
        nc.gpsimd.tensor_tensor(out=bv_a[:], in0=bv_all[:], in1=mul_a[:], op=ALU.mult)
        nc.vector.tensor_tensor(out=sh_g[:], in0=zs[2][:], in1=gate[:], op=ALU.mult)
        turn(1)
        multiply(0)
        quantise(1)
        for g in TURN_ORDER:
            turn(g)
            quantise(g)

        def turn_a():
            at_ps = ps_c.tile([P, 4, P], F32, name="at_ps", tag="c")
            for c in range(4):
                nc.tensor.transpose(at_ps[:, c, :], mul_a[:, P * c : P * (c + 1)], ident_f[:])
            nc.scalar.copy(out=at_sb[:], in_=at_ps[:])

        def finish_c():
            nc.gpsimd.tensor_tensor(out=add_c[:], in0=bv_a[:], in1=sh_g[:], op=ALU.add)
            ct_ps = ps_c.tile([P, 4, P], F32, name="ct_ps", tag="c")
            for c in range(4):
                nc.tensor.transpose(ct_ps[:, c, :], add_c[:, P * c : P * (c + 1)], ident_f[:])
            nc.scalar.copy(out=ct_sb[:], in_=ct_ps[:])
            c_ps = ps_c.tile([P, DO], F32, name="c_ps", tag="c")
            for c in range(4):
                nc.tensor.transpose(c_ps[:, P * c : P * (c + 1)], ct_sb[:, c, :], ident_f[:])
            return c_ps

        acc_ts = {}

        def unit_multiply(u):
            acc_t = ps_xt.tile([P, QUAD, P], F32, name="acc_t", tag="xt")
            nc.tensor.matmul_mx(
                out=acc_t[:].rearrange("p i b -> p (i b)"),
                lhsT=w_codes[:, P * u : P * (u + 1)].bitcast(FP8X4),
                lhsT_scale=w_scales[:, P * u : P * (u + 1)],
                rhs=quad_codes[:].bitcast(FP8X4),
                rhs_scale=quad_scales[:],
                start=True,
                stop=True,
            )
            acc_ts[u] = acc_t

        def unit_finish(u):
            prod_t = const.tile([P, QUAD, P], F32, name="prod_t%d" % u)
            nc.vector.tensor_tensor(
                out=prod_t[:],
                in0=acc_ts[u][:],
                in1=at_sb[:, u : u + 1, :].to_broadcast([P, QUAD, P]),
                op=ALU.mult,
            )
            back = ps_xt.tile([P, QUAD, P], F32, name="back", tag="xt")
            for i in range(QUAD):
                nc.tensor.matmul(
                    out=back[:, i, :], lhsT=ct_sb[:, u, :], rhs=ident_f[:],
                    is_transpose=True, start=True, stop=False,
                )
                nc.tensor.matmul(
                    out=back[:, i, :], lhsT=prod_t[:, i, :], rhs=ident_f[:],
                    is_transpose=True, start=False, stop=True,
                )
            res_t = const.tile([P, QUAD, P], F32, name="res_t%d" % u)
            nc.scalar.copy(out=res_t[:], in_=back[:])
            nc.scalar.dma_start(out=out[:, Q0 : Q0 + QUAD, P * u : P * (u + 1)], in_=res_t[:])

        turn_a()
        c_holder = []
        for g in range(NORMAL):
            if g + 1 < NORMAL:
                multiply(g + 1)
            u = g - FIRST_UNIT
            if u == -1:
                unit_multiply(0)
            if 0 <= u and u + 1 < 4:
                unit_multiply(u + 1)
            if 0 <= u and u < 4:
                unit_finish(u)
            for i2 in range(PAIR):
                i = PAIR * g + i2
                prod = const.tile([P, DO], F32, name="prod%d" % i)
                nc.vector.tensor_tensor(out=prod[:], in0=accs[i][:], in1=mul_a[:], op=ALU.mult)
                if i == 0:
                    c_holder.append(finish_c())
                res = const.tile([P, DO], F32, name="res%d" % i)
                if i == PAIR * NORMAL - 1:
                    for h in range(2):
                        cols = slice(DO // 2 * h, DO // 2 * (h + 1))
                        nc.vector.tensor_tensor(
                            out=res[:, cols], in0=prod[:, cols], in1=c_holder[0][:, cols], op=ALU.add
                        )
                        nc.sync.dma_start(out=out[:, i, cols], in_=res[:, cols])
                    continue
                if i in VEC_ADD:
                    nc.vector.tensor_tensor(out=res[:], in0=prod[:], in1=c_holder[0][:], op=ALU.add)
                else:
                    nc.gpsimd.tensor_tensor(out=res[:], in0=prod[:], in1=add_c[:], op=ALU.add)
                nc.sync.dma_start(out=out[:, i, :], in_=res[:])
